import numpy as np
import ml_dtypes

BF16 = ml_dtypes.bfloat16


def bf(x):
    return np.asarray(x, np.float32).astype(BF16)


def f32(x):
    return np.asarray(x, np.float32)


def f64(x):
    return np.asarray(x).astype(np.float64)


def striped(idx):
    return np.tile(idx.reshape(-1, 16).T, (8, 1))


C, S, K, M, N = 1024, 512, 29, 128, 14848


def setup_inputs():
    idx = np.concatenate([np.random.permutation(S) for _ in range(K)])
    return {"table": f32(np.random.standard_normal((C, S)) / np.sqrt(K)), "w2": bf(np.random.standard_normal((C, M)) / np.sqrt(C)), "b2": f32(0.1 * np.random.standard_normal((M, 1))), "offs": striped(idx)}


def reference(table, w2, b2, offs):
    idx = offs[:16].T.reshape(-1)
    t = f64(table)
    acc = np.zeros((C, S), np.float64)
    for k in range(K):
        acc = acc + t[:, idx[k * S:(k + 1) * S]]
    r = np.maximum(acc, 0.0)
    h = f64(w2).T @ r + f64(b2)
    return np.concatenate((np.maximum(h, 0.0), np.maximum(-h, 0.0)), axis=0)

@@ -1,0 +1,83 @@
+import concourse.mybir as mybir
+
+F32 = mybir.dt.float32
+BF16 = mybir.dt.bfloat16
+U16 = mybir.dt.uint16
+ADD = mybir.AluOpType.add
+MAX = mybir.AluOpType.max
+RELU = mybir.ActivationFunctionType.Relu
+
+P = 128
+CHANNELS = 1024
+WORDS = 512
+POSITIONS = 512
+SLOTS = 29
+HIDDEN = 128
+BLOCKS = CHANNELS // P
+RUN_COLUMNS = POSITIONS // 16
+PIECES = 2
+PIECE = POSITIONS // PIECES
+PIECE_COLUMNS = PIECE // 16
+
+FLOPS = 2 * CHANNELS * HIDDEN * POSITIONS
+
+
+def tile_silknnue_kernel(tc, table, w2, b2, offs, out):
+    nc = tc.nc
+    with (
+        tc.tile_pool(name="held", bufs=1) as held,
+        tc.tile_pool(name="sums", bufs=2) as sums,
+        tc.tile_pool(name="work", bufs=2) as work,
+        tc.psum_pool(name="psum", bufs=1) as psum,
+    ):
+        offsets = held.tile([P, SLOTS * RUN_COLUMNS], U16, name="offsets")
+        nc.sync.dma_start(offsets[:], offs)
+
+        windows = [held.tile([P, WORDS], F32, name=f"window{b}") for b in range(BLOCKS)]
+        for b in range(BLOCKS):
+            queue = nc.scalar if b % 2 == 0 else nc.sync
+            queue.dma_start(windows[b][:], table[b * P : (b + 1) * P, :])
+
+        weights = held.tile([P, BLOCKS, HIDDEN], BF16, name="weights")
+        nc.scalar.dma_start(weights[:], w2.rearrange("(b p) m -> p b m", p=P))
+        bias = held.tile([P, 1], F32, name="bias")
+        nc.scalar.dma_start(bias[:], b2)
+        minus_bias = held.tile([P, 1], F32, name="minus_bias")
+        nc.scalar.mul(minus_bias[:], bias[:], -1.0)
+
+        zero = held.tile([P, POSITIONS], F32, name="zero")
+        nc.vector.memset(zero[:], 0.0)
+
+        projected = [psum.tile([P, PIECE], F32, name=f"projected{q}") for q in range(PIECES)]
+        pieces = [slice(q * PIECE, (q + 1) * PIECE) for q in range(PIECES)]
+
+        acc = [zero for b in range(BLOCKS)]
+        for k in range(SLOTS):
+            first_column = k * RUN_COLUMNS
+            for b in range(BLOCKS):
+                so_far = acc[b]
+                acc[b] = sums.tile([P, POSITIONS], F32, name=f"acc{b}")
+                if (k, b) != (SLOTS - 1, BLOCKS - 1):
+                    run = offsets[:, first_column : first_column + RUN_COLUMNS]
+                    nc.vector.tensor_tensor(acc[b][:], windows[b][:].indirect(run), so_far[:], ADD)
+
+        for b in range(BLOCKS - 1):
+            r = work.tile([P, POSITIONS], BF16, name="r")
+            nc.scalar.activation(r[:], acc[b][:], RELU)
+            for q in range(PIECES):
+                nc.tensor.matmul(projected[q][:], weights[:, b, :], r[:, pieces[q]], start=(b == 0), stop=False)
+
+        b = BLOCKS - 1
+        plus = held.tile([P, POSITIONS], F32, name="plus")
+        minus = held.tile([P, POSITIONS], F32, name="minus")
+        for q in range(PIECES):
+            first_column = (SLOTS - 1) * RUN_COLUMNS + q * PIECE_COLUMNS
+            run = offsets[:, first_column : first_column + PIECE_COLUMNS]
+            nc.vector.tensor_tensor(acc[b][:, pieces[q]], windows[b][:].indirect(run), so_far[:, pieces[q]], ADD)
+            r_piece = work.tile([P, PIECE], BF16, name="r_piece")
+            nc.vector.tensor_scalar_max(r_piece[:], acc[b][:, pieces[q]], 0.0)
+            nc.tensor.matmul(projected[q][:], weights[:, b, :], r_piece[:], start=False, stop=True)
+            nc.vector.tensor_scalar(plus[:, pieces[q]], projected[q][:], bias[:], 0.0, ADD, MAX)
+            nc.sync.dma_start(out[0:HIDDEN, pieces[q]], plus[:, pieces[q]])
+            nc.scalar.activation(minus[:, pieces[q]], projected[q][:], RELU, bias=minus_bias[:], scale=-1.0)
+            nc.sync.dma_start(out[HIDDEN : 2 * HIDDEN, pieces[q]], minus[:, pieces[q]])

@@ -15,9 +15,10 @@ SLOTS = 29
 HIDDEN = 128
 BLOCKS = CHANNELS // P
 RUN_COLUMNS = POSITIONS // 16
-PIECES = 2
-PIECE = POSITIONS // PIECES
-PIECE_COLUMNS = PIECE // 16
+LATE_BLOCKS = 2
+LATE_SLOTS = 2
+EARLY_BLOCKS = BLOCKS - LATE_BLOCKS
+FIRST_PIECE = 320
 
 FLOPS = 2 * CHANNELS * HIDDEN * POSITIONS
 
@@ -48,36 +49,47 @@ def tile_silknnue_kernel(tc, table, w2, b2, offs, out):
         zero = held.tile([P, POSITIONS], F32, name="zero")
         nc.vector.memset(zero[:], 0.0)
 
-        projected = [psum.tile([P, PIECE], F32, name=f"projected{q}") for q in range(PIECES)]
-        pieces = [slice(q * PIECE, (q + 1) * PIECE) for q in range(PIECES)]
+        pieces = [slice(0, FIRST_PIECE), slice(FIRST_PIECE, POSITIONS)]
+        widths = [FIRST_PIECE, POSITIONS - FIRST_PIECE]
+        projected = [psum.tile([P, widths[q]], F32, name=f"projected{q}") for q in range(2)]
 
         acc = [zero for b in range(BLOCKS)]
         for k in range(SLOTS):
-            first_column = k * RUN_COLUMNS
-            for b in range(BLOCKS):
+            run = offsets[:, k * RUN_COLUMNS : (k + 1) * RUN_COLUMNS]
+            for b in range(BLOCKS if k < SLOTS - LATE_SLOTS else EARLY_BLOCKS):
                 so_far = acc[b]
                 acc[b] = sums.tile([P, POSITIONS], F32, name=f"acc{b}")
-                if (k, b) != (SLOTS - 1, BLOCKS - 1):
-                    run = offsets[:, first_column : first_column + RUN_COLUMNS]
-                    nc.vector.tensor_tensor(acc[b][:], windows[b][:].indirect(run), so_far[:], ADD)
+                nc.vector.tensor_tensor(acc[b][:], windows[b][:].indirect(run), so_far[:], ADD)
 
-        for b in range(BLOCKS - 1):
+        for b in range(EARLY_BLOCKS):
             r = work.tile([P, POSITIONS], BF16, name="r")
             nc.scalar.activation(r[:], acc[b][:], RELU)
-            for q in range(PIECES):
+            for q in range(2):
                 nc.tensor.matmul(projected[q][:], weights[:, b, :], r[:, pieces[q]], start=(b == 0), stop=False)
 
-        b = BLOCKS - 1
         plus = held.tile([P, POSITIONS], F32, name="plus")
         minus = held.tile([P, POSITIONS], F32, name="minus")
-        for q in range(PIECES):
-            first_column = (SLOTS - 1) * RUN_COLUMNS + q * PIECE_COLUMNS
-            run = offsets[:, first_column : first_column + PIECE_COLUMNS]
-            nc.vector.tensor_tensor(acc[b][:, pieces[q]], windows[b][:].indirect(run), so_far[:, pieces[q]], ADD)
-            r_piece = work.tile([P, PIECE], BF16, name="r_piece")
-            nc.vector.tensor_scalar_max(r_piece[:], acc[b][:, pieces[q]], 0.0)
-            nc.tensor.matmul(projected[q][:], weights[:, b, :], r_piece[:], start=False, stop=True)
-            nc.vector.tensor_scalar(plus[:, pieces[q]], projected[q][:], bias[:], 0.0, ADD, MAX)
+        for q in range(2):
+            late = {b: acc[b][:, pieces[q]] for b in range(EARLY_BLOCKS, BLOCKS)}
+            for k in range(SLOTS - LATE_SLOTS, SLOTS):
+                first_column = (k * POSITIONS + pieces[q].start) // 16
+                run = offsets[:, first_column : first_column + widths[q] // 16]
+                for b in range(EARLY_BLOCKS, BLOCKS):
+                    so_far = late[b]
+                    late_sum = held.tile([P, widths[q]], F32, name=f"late{b}_{k}_{q}")
+                    late[b] = late_sum[:]
+                    nc.vector.tensor_tensor(late[b], windows[b][:].indirect(run), so_far, ADD)
+            for b in range(EARLY_BLOCKS, BLOCKS):
+                r_piece = work.tile([P, widths[q]], BF16, name=f"r_piece{q}")
+                if q == 0:
+                    nc.scalar.activation(r_piece[:], late[b], RELU)
+                else:
+                    nc.vector.tensor_scalar_max(r_piece[:], late[b], 0.0)
+                nc.tensor.matmul(projected[q][:], weights[:, b, :], r_piece[:], start=False, stop=(b == BLOCKS - 1))
+            if q == 0:
+                nc.scalar.activation(plus[:, pieces[q]], projected[q][:], RELU, bias=bias[:])
+            else:
+                nc.vector.tensor_scalar(plus[:, pieces[q]], projected[q][:], bias[:], 0.0, ADD, MAX)
             nc.sync.dma_start(out[0:HIDDEN, pieces[q]], plus[:, pieces[q]])
             nc.scalar.activation(minus[:, pieces[q]], projected[q][:], RELU, bias=minus_bias[:], scale=-1.0)
             nc.sync.dma_start(out[HIDDEN : 2 * HIDDEN, pieces[q]], minus[:, pieces[q]])

@@ -16,9 +16,9 @@ HIDDEN = 128
 BLOCKS = CHANNELS // P
 RUN_COLUMNS = POSITIONS // 16
 LATE_BLOCKS = 2
-LATE_SLOTS = 2
+LATE_SLOTS = 3
 EARLY_BLOCKS = BLOCKS - LATE_BLOCKS
-FIRST_PIECE = 320
+FIRST_PIECE = 384
 
 FLOPS = 2 * CHANNELS * HIDDEN * POSITIONS
 

import concourse.mybir as mybir

F32 = mybir.dt.float32
BF16 = mybir.dt.bfloat16
U16 = mybir.dt.uint16
ADD = mybir.AluOpType.add
MAX = mybir.AluOpType.max
RELU = mybir.ActivationFunctionType.Relu

P = 128
CHANNELS = 1024
WORDS = 512
POSITIONS = 512
SLOTS = 29
HIDDEN = 128
BLOCKS = CHANNELS // P
RUN_COLUMNS = POSITIONS // 16
LATE_BLOCKS = 2
LATE_SLOTS = 3
EARLY_BLOCKS = BLOCKS - LATE_BLOCKS
FIRST_PIECE = 384

FLOPS = 2 * CHANNELS * HIDDEN * POSITIONS


def tile_silknnue_kernel(tc, table, w2, b2, offs, out):
    nc = tc.nc
    with (
        tc.tile_pool(name="held", bufs=1) as held,
        tc.tile_pool(name="sums", bufs=2) as sums,
        tc.tile_pool(name="work", bufs=2) as work,
        tc.psum_pool(name="psum", bufs=1) as psum,
    ):
        offsets = held.tile([P, SLOTS * RUN_COLUMNS], U16, name="offsets")
        nc.sync.dma_start(offsets[:], offs)

        windows = [held.tile([P, WORDS], F32, name=f"window{b}") for b in range(BLOCKS)]
        for b in range(BLOCKS):
            queue = nc.scalar if b % 2 == 0 else nc.sync
            queue.dma_start(windows[b][:], table[b * P : (b + 1) * P, :])

        weights = held.tile([P, BLOCKS, HIDDEN], BF16, name="weights")
        nc.scalar.dma_start(weights[:], w2.rearrange("(b p) m -> p b m", p=P))
        bias = held.tile([P, 1], F32, name="bias")
        nc.scalar.dma_start(bias[:], b2)
        minus_bias = held.tile([P, 1], F32, name="minus_bias")
        nc.scalar.mul(minus_bias[:], bias[:], -1.0)

        zero = held.tile([P, POSITIONS], F32, name="zero")
        nc.vector.memset(zero[:], 0.0)

        pieces = [slice(0, FIRST_PIECE), slice(FIRST_PIECE, POSITIONS)]
        widths = [FIRST_PIECE, POSITIONS - FIRST_PIECE]
        projected = [psum.tile([P, widths[q]], F32, name=f"projected{q}") for q in range(2)]

        acc = [zero for b in range(BLOCKS)]
        for k in range(SLOTS):
            run = offsets[:, k * RUN_COLUMNS : (k + 1) * RUN_COLUMNS]
            for b in range(BLOCKS if k < SLOTS - LATE_SLOTS else EARLY_BLOCKS):
                so_far = acc[b]
                acc[b] = sums.tile([P, POSITIONS], F32, name=f"acc{b}")
                nc.vector.tensor_tensor(acc[b][:], windows[b][:].indirect(run), so_far[:], ADD)

        for b in range(EARLY_BLOCKS):
            r = work.tile([P, POSITIONS], BF16, name="r")
            nc.scalar.activation(r[:], acc[b][:], RELU)
            for q in range(2):
                nc.tensor.matmul(projected[q][:], weights[:, b, :], r[:, pieces[q]], start=(b == 0), stop=False)

        plus = held.tile([P, POSITIONS], F32, name="plus")
        minus = held.tile([P, POSITIONS], F32, name="minus")
        for q in range(2):
            late = {b: acc[b][:, pieces[q]] for b in range(EARLY_BLOCKS, BLOCKS)}
            for k in range(SLOTS - LATE_SLOTS, SLOTS):
                first_column = (k * POSITIONS + pieces[q].start) // 16
                run = offsets[:, first_column : first_column + widths[q] // 16]
                for b in range(EARLY_BLOCKS, BLOCKS):
                    so_far = late[b]
                    late_sum = held.tile([P, widths[q]], F32, name=f"late{b}_{k}_{q}")
                    late[b] = late_sum[:]
                    nc.vector.tensor_tensor(late[b], windows[b][:].indirect(run), so_far, ADD)
            for b in range(EARLY_BLOCKS, BLOCKS):
                r_piece = work.tile([P, widths[q]], BF16, name=f"r_piece{q}")
                if q == 0:
                    nc.scalar.activation(r_piece[:], late[b], RELU)
                else:
                    nc.vector.tensor_scalar_max(r_piece[:], late[b], 0.0)
                nc.tensor.matmul(projected[q][:], weights[:, b, :], r_piece[:], start=False, stop=(b == BLOCKS - 1))
            if q == 0:
                nc.scalar.activation(plus[:, pieces[q]], projected[q][:], RELU, bias=bias[:])
            else:
                nc.vector.tensor_scalar(plus[:, pieces[q]], projected[q][:], bias[:], 0.0, ADD, MAX)
            nc.sync.dma_start(out[0:HIDDEN, pieces[q]], plus[:, pieces[q]])
            nc.scalar.activation(minus[:, pieces[q]], projected[q][:], RELU, bias=minus_bias[:], scale=-1.0)
            nc.sync.dma_start(out[HIDDEN : 2 * HIDDEN, pieces[q]], minus[:, pieces[q]])
